import numpy as np
import ml_dtypes


def mxq(x, axis, fmt="e4m3"):
    dtype, down = {"e4m3": (ml_dtypes.float8_e4m3fn, 7), "e5m2": (ml_dtypes.float8_e5m2, 14)}[fmt]
    v = np.moveaxis(np.asarray(x, np.float32).astype(ml_dtypes.bfloat16).astype(np.float64), axis, -1)
    blocks = v.reshape(v.shape[:-1] + (-1, 32))
    amax = np.abs(blocks).max(-1, keepdims=True)
    byte = np.maximum(np.where(amax > 0, np.frexp(amax)[1] - 1 + 127, 0) - down, 1)
    scale = np.exp2(byte - 127.0)
    codes = (blocks / scale).astype(np.float32).astype(dtype).astype(np.float64)
    return np.moveaxis((codes * scale).reshape(v.shape), -1, axis)


WIDE = False


def mx_kscale(k):
    if not WIDE:
        return np.ones(k)
    levels = np.array([10, -10, 5, -5, 0])
    a = np.random.permutation(np.resize(levels, k // 512 * 4)).reshape(k // 512, 4)
    idx = np.arange(k)
    return np.exp2(a[idx // 512, idx % 128 // 32])


BF16 = ml_dtypes.bfloat16


def bf(x):
    return np.asarray(x, np.float32).astype(BF16)


def f64(x):
    return np.asarray(x).astype(np.float64)


B, A, S, R, H = 512, 32, 512, 1024, 1024


def elu(v):
    return np.where(v > 0.0, v, np.exp(np.minimum(v, 0.0)) - 1.0)


def softplus(v):
    return np.maximum(v, 0.0) + np.log(1.0 + np.exp(-np.abs(v)))


def setup_inputs():
    s = mx_kscale(R)
    return {"rnn_hidden": bf(np.random.standard_normal((B, R)) * 0.7 * s),
            "eps": bf(np.random.standard_normal((B, S))),
            "W_h": bf(np.random.standard_normal((H, R)) * 1.4 / np.sqrt(R) / s[None, :]),
            "b_h": bf(np.random.standard_normal(H) * 0.3),
            "W_out": bf(np.random.standard_normal((2 * S, H)) * 1.5 / np.sqrt(H)),
            "b_out": bf(np.random.standard_normal(2 * S) * 0.3)}


def reference(rnn_hidden, eps, W_h, b_h, W_out, b_out):
    h2 = elu((mxq(f64(rnn_hidden), 1, "e4m3") @ mxq(f64(W_h), 1, "e4m3").T) + f64(b_h))
    o = (mxq(h2, 1, "e4m3") @ mxq(f64(W_out), 1, "e4m3").T) + f64(b_out)
    mean, std_pre = np.split(o, 2, axis=-1)
    std = softplus(std_pre) + 0.1
    new_sample = mean + std * f64(eps)
    return (mean, std, new_sample)

@@ -1,0 +1,229 @@
+import math
+from contextlib import ExitStack
+
+import concourse.mybir as mybir
+from concourse.masks import make_identity
+
+F32 = mybir.dt.float32
+BF16 = mybir.dt.bfloat16
+U32 = mybir.dt.uint32
+U8 = mybir.dt.uint8
+FP8X4 = mybir.dt.float8_e4m3fn_x4
+ACT = mybir.ActivationFunctionType
+ALU = mybir.AluOpType
+
+P = 128
+PACK = 4
+BATCH = 512
+DEPTH = 1024
+HIDDEN = 1024
+SAMPLE = 512
+PASSES = DEPTH // (P * PACK)
+CHUNKS = DEPTH // 2 // P
+BATCH_TILES = BATCH // P
+HIDDEN_TILES = HIDDEN // P
+MEAN = 0
+STD = 1
+
+FLOPS = 2 * BATCH * DEPTH * HIDDEN + 2 * BATCH * DEPTH * 2 * SAMPLE
+
+
+def turn_row_tile(nc, banks, identity, rows):
+    words = rows.bitcast(F32)
+    turned = banks.tile([P, CHUNKS, P], F32, tag="turned")
+    for c in range(CHUNKS):
+        nc.tensor.transpose(turned[:, c, :], words[:, c * P : (c + 1) * P], identity[:])
+    return turned
+
+
+def by_pass_and_column(turned):
+    return turned[:].rearrange("p (g u) r -> p g r u", u=2)
+
+
+def words_view(grouped):
+    return grouped[:].bitcast(F32).rearrange("p (g n u) -> p g n u", g=PASSES, u=2)
+
+
+def tile_prior_pb_kernel(
+    tc, rnn_hidden, eps, W_h, b_h, W_out, b_out, out_0, out_1, out_2
+):
+    nc = tc.nc
+    with ExitStack() as ctx:
+        keep = ctx.enter_context(tc.tile_pool(name="keep", bufs=1))
+        stage = ctx.enter_context(tc.tile_pool(name="stage", bufs=3))
+        banks = ctx.enter_context(tc.psum_pool(name="banks", bufs=4))
+        sums = ctx.enter_context(tc.psum_pool(name="sums", bufs=4))
+
+        identity = keep.tile([P, P], F32)
+        make_identity(nc, identity[:])
+        warm = keep.tile([P, 1], F32)
+        nc.vector.memset(warm[:], 0.0)
+        nc.scalar.activation(out=warm[:], in_=warm[:], func=ACT.Exp)
+
+        x_rows = keep.tile([P, BATCH_TILES, DEPTH], BF16)
+        x_dram = rnn_hidden.rearrange("(p i) r -> p i r", i=BATCH_TILES)
+        for j in range(2):
+            nc.sync.dma_start(out=x_rows[:, 2 * j : 2 * j + 2, :], in_=x_dram[:, 2 * j : 2 * j + 2, :])
+
+        wh_rows = keep.tile([P, HIDDEN_TILES, DEPTH], BF16)
+        wh_dram = W_h.rearrange("(c p e) r -> p c e r", p=P, e=2)
+        bh_bf16 = keep.tile([P, HIDDEN_TILES], BF16)
+        nc.scalar.dma_start(
+            out=bh_bf16[:].rearrange("p (c e) -> p c e", e=2),
+            in_=b_h.rearrange("(c p e) -> p c e", p=P, e=2),
+        )
+        for c in range(HIDDEN_TILES // 2):
+            nc.sync.dma_start(out=wh_rows[:, 2 * c : 2 * c + 2, :], in_=wh_dram[:, c, :, :])
+
+        wo_rows = keep.tile([P, 2 * SAMPLE // P, DEPTH], BF16)
+        wo_dram = W_out.rearrange("(c p) h -> p c h", p=P)
+        for half in (STD, MEAN):
+            for j in range(2):
+                c = 4 * half + 2 * j
+                nc.sync.dma_start(out=wo_rows[:, c : c + 2, :], in_=wo_dram[:, c : c + 2, :])
+        eps_rows = keep.tile([P, BATCH_TILES, SAMPLE], BF16)
+        nc.sync.dma_start(out=eps_rows[:], in_=eps.rearrange("(p i) s -> p i s", i=BATCH_TILES))
+        bo_all = keep.tile([P, 2 * SAMPLE], BF16)
+        nc.sync.dma_start(out=bo_all[:], in_=b_out.partition_broadcast(P))
+
+        bh = keep.tile([P, HIDDEN_TILES], F32)
+        nc.vector.tensor_copy(out=bh[:], in_=bh_bf16[:])
+
+        x_grouped = keep.tile([P, PASSES * BATCH * PACK], BF16, align_bytes=64)
+        x_codes = keep.tile([P, PASSES, BATCH], U32, align_bytes=64)
+        x_scales = keep.tile([P, PASSES, BATCH], U8, align_bytes=64)
+        for i in range(BATCH_TILES):
+            turned = turn_row_tile(nc, banks, identity, x_rows[:, i, :])
+            copy_out = nc.scalar.copy if i % 2 == 0 else nc.vector.tensor_copy
+            copy_out(
+                out=words_view(x_grouped)[:, :, i * P : (i + 1) * P, :],
+                in_=by_pass_and_column(turned),
+            )
+        for g in range(PASSES):
+            nc.vector.quantize_mx(
+                out=x_codes[:, g, :].bitcast(FP8X4),
+                scales=x_scales[:, g, :],
+                in_=x_grouped[:, g * BATCH * PACK : (g + 1) * BATCH * PACK],
+            )
+
+        wh_codes = keep.tile([P, HIDDEN_TILES, PASSES * P], U32, align_bytes=64)
+        wh_scales = keep.tile([P, HIDDEN_TILES, PASSES * P], U8, align_bytes=64)
+        h2_codes = keep.tile([P, PASSES, BATCH], U32, align_bytes=64)
+        h2_scales = keep.tile([P, PASSES, BATCH], U8, align_bytes=64)
+        for g2 in range(PASSES):
+            h2_rows = stage.tile([P, PACK, BATCH], BF16, bufs=2)
+            for t in range(PACK):
+                m = PACK * g2 + t
+                turned = turn_row_tile(nc, banks, identity, wh_rows[:, m, :])
+                wh_grouped = stage.tile([P, PASSES * P * PACK], BF16, align_bytes=64)
+                nc.scalar.copy(out=words_view(wh_grouped), in_=by_pass_and_column(turned))
+                nc.vector.quantize_mx(
+                    out=wh_codes[:, m, :].bitcast(FP8X4),
+                    scales=wh_scales[:, m, :],
+                    in_=wh_grouped[:],
+                )
+                pre_h = sums.tile([P, BATCH], F32, tag="sum")
+                for g in range(PASSES):
+                    nc.tensor.matmul_mx(
+                        out=pre_h[:],
+                        lhsT=wh_codes[:, m, g * P : (g + 1) * P].bitcast(FP8X4),
+                        lhsT_scale=wh_scales[:, m, g * P : (g + 1) * P],
+                        rhs=x_codes[:, g, :].bitcast(FP8X4),
+                        rhs_scale=x_scales[:, g, :],
+                        start=(g == 0),
+                        stop=(g == PASSES - 1),
+                    )
+                below = stage.tile([P, BATCH], F32)
+                nc.scalar.activation(out=below[:], in_=pre_h[:], func=ACT.Exp, bias=bh[:, m : m + 1])
+                nc.vector.tensor_scalar(
+                    out=below[:], in0=below[:], scalar1=-1.0, scalar2=0.0, op0=ALU.add, op1=ALU.min
+                )
+                nc.vector.scalar_tensor_tensor(
+                    out=h2_rows[:, t, :],
+                    in0=pre_h[:],
+                    scalar=bh[:, m : m + 1],
+                    in1=below[:],
+                    op0=ALU.add,
+                    op1=ALU.max,
+                )
+            h2_grouped = stage.tile([P, BATCH, PACK], BF16, bufs=2, align_bytes=64)
+            nc.vector.tensor_copy(out=h2_grouped[:], in_=h2_rows[:].rearrange("p t b -> p b t"))
+            nc.vector.quantize_mx(
+                out=h2_codes[:, g2, :].bitcast(FP8X4),
+                scales=h2_scales[:, g2, :],
+                in_=h2_grouped[:].rearrange("p b t -> p (b t)"),
+            )
+
+        wo_codes = keep.tile([P, 2, PASSES, SAMPLE], U32, align_bytes=64)
+        wo_scales = keep.tile([P, 2, PASSES, SAMPLE], U8, align_bytes=64)
+
+        def quantise_wo(half):
+            wo_grouped = stage.tile([P, PASSES * SAMPLE * PACK], BF16, bufs=2, align_bytes=64)
+            for j in range(SAMPLE // P):
+                turned = turn_row_tile(nc, banks, identity, wo_rows[:, 4 * half + j, :])
+                nc.scalar.copy(
+                    out=words_view(wo_grouped)[:, :, j * P : (j + 1) * P, :],
+                    in_=by_pass_and_column(turned),
+                )
+            for g in range(PASSES):
+                nc.vector.quantize_mx(
+                    out=wo_codes[:, half, g, :].bitcast(FP8X4),
+                    scales=wo_scales[:, half, g, :],
+                    in_=wo_grouped[:, g * SAMPLE * PACK : (g + 1) * SAMPLE * PACK],
+                )
+
+        def second_product(half, i):
+            o_sum = sums.tile([P, SAMPLE], F32, tag="sum")
+            for g in range(PASSES):
+                nc.tensor.matmul_mx(
+                    out=o_sum[:],
+                    lhsT=h2_codes[:, g, i * P : (i + 1) * P].bitcast(FP8X4),
+                    lhsT_scale=h2_scales[:, g, i * P : (i + 1) * P],
+                    rhs=wo_codes[:, half, g, :].bitcast(FP8X4),
+                    rhs_scale=wo_scales[:, half, g, :],
+                    start=(g == 0),
+                    stop=(g == PASSES - 1),
+                )
+            return o_sum
+
+        mean = keep.tile([P, BATCH_TILES, SAMPLE], F32)
+        std_pre = keep.tile([P, BATCH_TILES, SAMPLE], F32)
+        soft = keep.tile([P, BATCH_TILES, SAMPLE], F32)
+        std = keep.tile([P, BATCH_TILES, SAMPLE], F32)
+        sample = keep.tile([P, BATCH_TILES, SAMPLE], F32)
+        mean_dram = out_0.rearrange("(p i) s -> p i s", i=BATCH_TILES)
+        std_dram = out_1.rearrange("(p i) s -> p i s", i=BATCH_TILES)
+        sample_dram = out_2.rearrange("(p i) s -> p i s", i=BATCH_TILES)
+
+        quantise_wo(STD)
+        for i in range(BATCH_TILES):
+            o_sum = second_product(STD, i)
+            nc.vector.tensor_tensor(
+                out=std_pre[:, i, :], in0=o_sum[:], in1=bo_all[:, SAMPLE : 2 * SAMPLE], op=ALU.add
+            )
+            nc.scalar.activation(out=soft[:, i, :], in_=std_pre[:, i, :], func=ACT.Abs)
+            nc.scalar.activation(out=soft[:, i, :], in_=soft[:, i, :], func=ACT.Exp, scale=-1.0)
+
+        quantise_wo(MEAN)
+        for i in range(BATCH_TILES):
+            o_sum = second_product(MEAN, i)
+            nc.vector.tensor_tensor(out=mean[:, i, :], in0=o_sum[:], in1=bo_all[:, 0:SAMPLE], op=ALU.add)
+            nc.sync.dma_start(out=mean_dram[:, i, :], in_=mean[:, i, :])
+
+        c_tenth = math.exp(0.1)
+        for i in range(BATCH_TILES):
+            nc.scalar.activation(
+                out=soft[:, i, :], in_=soft[:, i, :], func=ACT.Ln, scale=c_tenth, bias=c_tenth
+            )
+            nc.vector.scalar_tensor_tensor(
+                out=std[:, i, :],
+                in0=std_pre[:, i, :],
+                scalar=0.0,
+                in1=soft[:, i, :],
+                op0=ALU.max,
+                op1=ALU.add,
+            )
+            nc.sync.dma_start(out=std_dram[:, i, :], in_=std[:, i, :])
+            nc.vector.tensor_tensor(out=sample[:, i, :], in0=std[:, i, :], in1=eps_rows[:, i, :], op=ALU.mult)
+            nc.vector.tensor_tensor(out=sample[:, i, :], in0=sample[:, i, :], in1=mean[:, i, :], op=ALU.add)
+            nc.sync.dma_start(out=sample_dram[:, i, :], in_=sample[:, i, :])

@@ -22,26 +22,24 @@ PASSES = DEPTH // (P * PACK)
 CHUNKS = DEPTH // 2 // P
 BATCH_TILES = BATCH // P
 HIDDEN_TILES = HIDDEN // P
+WH_CHUNKS = HIDDEN_TILES // 2
+WH_AHEAD = 2
 MEAN = 0
 STD = 1
 
 FLOPS = 2 * BATCH * DEPTH * HIDDEN + 2 * BATCH * DEPTH * 2 * SAMPLE
 
 
-def turn_row_tile(nc, banks, identity, rows):
+def turn_row_tile(nc, banks, identity, rows, grouped_words, copy_out):
     words = rows.bitcast(F32)
     turned = banks.tile([P, CHUNKS, P], F32, tag="turned")
     for c in range(CHUNKS):
         nc.tensor.transpose(turned[:, c, :], words[:, c * P : (c + 1) * P], identity[:])
-    return turned
-
-
-def by_pass_and_column(turned):
-    return turned[:].rearrange("p (g u) r -> p g r u", u=2)
+    copy_out(out=grouped_words, in_=turned[:].rearrange("p (g u) r -> p g r u", u=2))
 
 
 def words_view(grouped):
-    return grouped[:].bitcast(F32).rearrange("p (g n u) -> p g n u", g=PASSES, u=2)
+    return grouped.bitcast(F32).rearrange("p (g n u) -> p g n u", g=PASSES, u=2)
 
 
 def tile_prior_pb_kernel(
@@ -50,9 +48,10 @@ def tile_prior_pb_kernel(
     nc = tc.nc
     with ExitStack() as ctx:
         keep = ctx.enter_context(tc.tile_pool(name="keep", bufs=1))
-        stage = ctx.enter_context(tc.tile_pool(name="stage", bufs=3))
+        stage = ctx.enter_context(tc.tile_pool(name="stage", bufs=2))
         banks = ctx.enter_context(tc.psum_pool(name="banks", bufs=4))
         sums = ctx.enter_context(tc.psum_pool(name="sums", bufs=4))
+        ctx.enter_context(tc.manual_schedule())
 
         identity = keep.tile([P, P], F32)
         make_identity(nc, identity[:])
@@ -72,32 +71,31 @@ def tile_prior_pb_kernel(
             out=bh_bf16[:].rearrange("p (c e) -> p c e", e=2),
             in_=b_h.rearrange("(c p e) -> p c e", p=P, e=2),
         )
-        for c in range(HIDDEN_TILES // 2):
+        for c in range(WH_CHUNKS):
             nc.sync.dma_start(out=wh_rows[:, 2 * c : 2 * c + 2, :], in_=wh_dram[:, c, :, :])
 
-        wo_rows = keep.tile([P, 2 * SAMPLE // P, DEPTH], BF16)
-        wo_dram = W_out.rearrange("(c p) h -> p c h", p=P)
+        wo_rows = keep.tile([P, 2, SAMPLE // P, DEPTH], BF16)
+        wo_dram = W_out.rearrange("(f j p) h -> p f j h", f=2, p=P)
         for half in (STD, MEAN):
             for j in range(2):
-                c = 4 * half + 2 * j
-                nc.sync.dma_start(out=wo_rows[:, c : c + 2, :], in_=wo_dram[:, c : c + 2, :])
+                nc.sync.dma_start(
+                    out=wo_rows[:, half, 2 * j : 2 * j + 2, :], in_=wo_dram[:, half, 2 * j : 2 * j + 2, :]
+                )
         eps_rows = keep.tile([P, BATCH_TILES, SAMPLE], BF16)
         nc.sync.dma_start(out=eps_rows[:], in_=eps.rearrange("(p i) s -> p i s", i=BATCH_TILES))
-        bo_all = keep.tile([P, 2 * SAMPLE], BF16)
-        nc.sync.dma_start(out=bo_all[:], in_=b_out.partition_broadcast(P))
+        bo_all = keep.tile([P, 2, SAMPLE], BF16)
+        nc.sync.dma_start(out=bo_all[:].rearrange("p f s -> p (f s)"), in_=b_out.partition_broadcast(P))
 
-        bh = keep.tile([P, HIDDEN_TILES], F32)
-        nc.vector.tensor_copy(out=bh[:], in_=bh_bf16[:])
+        both = (nc.scalar.copy, nc.vector.tensor_copy)
+        scalar_only = (nc.scalar.copy, nc.scalar.copy)
 
         x_grouped = keep.tile([P, PASSES * BATCH * PACK], BF16, align_bytes=64)
         x_codes = keep.tile([P, PASSES, BATCH], U32, align_bytes=64)
         x_scales = keep.tile([P, PASSES, BATCH], U8, align_bytes=64)
         for i in range(BATCH_TILES):
-            turned = turn_row_tile(nc, banks, identity, x_rows[:, i, :])
-            copy_out = nc.scalar.copy if i % 2 == 0 else nc.vector.tensor_copy
-            copy_out(
-                out=words_view(x_grouped)[:, :, i * P : (i + 1) * P, :],
-                in_=by_pass_and_column(turned),
+            turn_row_tile(
+                nc, banks, identity, x_rows[:, i, :],
+                words_view(x_grouped[:])[:, :, i * P : (i + 1) * P, :], both[i % 2],
             )
         for g in range(PASSES):
             nc.vector.quantize_mx(
@@ -106,71 +104,102 @@ def tile_prior_pb_kernel(
                 in_=x_grouped[:, g * BATCH * PACK : (g + 1) * BATCH * PACK],
             )
 
+        bh = keep.tile([P, HIDDEN_TILES], F32)
+        nc.vector.tensor_copy(out=bh[:], in_=bh_bf16[:])
+
         wh_codes = keep.tile([P, HIDDEN_TILES, PASSES * P], U32, align_bytes=64)
         wh_scales = keep.tile([P, HIDDEN_TILES, PASSES * P], U8, align_bytes=64)
+
+        def turn_wh(c, copiers):
+            wh_grouped = stage.tile([P, 2, PASSES * P * PACK], BF16, align_bytes=64)
+            for e in range(2):
+                turn_row_tile(
+                    nc, banks, identity, wh_rows[:, 2 * c + e, :], words_view(wh_grouped[:, e, :]), copiers[e]
+                )
+            return wh_grouped
+
+        def quantise_wh(c, wh_grouped):
+            nc.vector.quantize_mx(
+                out=wh_codes[:, 2 * c : 2 * c + 2, :].rearrange("p e n -> p (e n)").bitcast(FP8X4),
+                scales=wh_scales[:, 2 * c : 2 * c + 2, :].rearrange("p e n -> p (e n)"),
+                in_=wh_grouped[:].rearrange("p e n -> p (e n)"),
+            )
+
+        wo_grouped = keep.tile([P, 2, PASSES * SAMPLE * PACK], BF16, align_bytes=64)
+        wo_codes = keep.tile([P, 2, PASSES, SAMPLE], U32, align_bytes=64)
+        wo_scales = keep.tile([P, 2, PASSES, SAMPLE], U8, align_bytes=64)
+
+        def turn_wo(half, j):
+            turn_row_tile(
+                nc, banks, identity, wo_rows[:, half, j, :],
+                words_view(wo_grouped[:, half, :])[:, :, j * P : (j + 1) * P, :], nc.scalar.copy,
+            )
+
+        def quantise_wo(half):
+            for g in range(PASSES):
+                nc.vector.quantize_mx(
+                    out=wo_codes[:, half, g, :].bitcast(FP8X4),
+                    scales=wo_scales[:, half, g, :],
+                    in_=wo_grouped[:, half, g * SAMPLE * PACK : (g + 1) * SAMPLE * PACK],
+                )
+
         h2_codes = keep.tile([P, PASSES, BATCH], U32, align_bytes=64)
         h2_scales = keep.tile([P, PASSES, BATCH], U8, align_bytes=64)
-        for g2 in range(PASSES):
-            h2_rows = stage.tile([P, PACK, BATCH], BF16, bufs=2)
-            for t in range(PACK):
-                m = PACK * g2 + t
-                turned = turn_row_tile(nc, banks, identity, wh_rows[:, m, :])
-                wh_grouped = stage.tile([P, PASSES * P * PACK], BF16, align_bytes=64)
-                nc.scalar.copy(out=words_view(wh_grouped), in_=by_pass_and_column(turned))
-                nc.vector.quantize_mx(
-                    out=wh_codes[:, m, :].bitcast(FP8X4),
-                    scales=wh_scales[:, m, :],
-                    in_=wh_grouped[:],
-                )
-                pre_h = sums.tile([P, BATCH], F32, tag="sum")
-                for g in range(PASSES):
-                    nc.tensor.matmul_mx(
-                        out=pre_h[:],
-                        lhsT=wh_codes[:, m, g * P : (g + 1) * P].bitcast(FP8X4),
-                        lhsT_scale=wh_scales[:, m, g * P : (g + 1) * P],
-                        rhs=x_codes[:, g, :].bitcast(FP8X4),
-                        rhs_scale=x_scales[:, g, :],
-                        start=(g == 0),
-                        stop=(g == PASSES - 1),
-                    )
-                below = stage.tile([P, BATCH], F32)
-                nc.scalar.activation(out=below[:], in_=pre_h[:], func=ACT.Exp, bias=bh[:, m : m + 1])
+
+        def hidden_pass(g2, half):
+            h2_rows = stage.tile([P, PACK, BATCH], BF16)
+            for u2 in range(2):
+                c = 2 * g2 + u2
+                below = stage.tile([P, 2, BATCH], F32)
+                pre_hs = []
+                for e in range(2):
+                    m = 2 * c + e
+                    pre_h = sums.tile([P, BATCH], F32, tag="sum")
+                    pre_hs.append(pre_h)
+                    for g in range(PASSES):
+                        nc.tensor.matmul_mx(
+                            out=pre_h[:],
+                            lhsT=wh_codes[:, m, g * P : (g + 1) * P].bitcast(FP8X4),
+                            lhsT_scale=wh_scales[:, m, g * P : (g + 1) * P],
+                            rhs=x_codes[:, g, :].bitcast(FP8X4),
+                            rhs_scale=x_scales[:, g, :],
+                            start=(g == 0),
+                            stop=(g == PASSES - 1),
+                        )
+                    nc.scalar.activation(out=below[:, e, :], in_=pre_h[:], func=ACT.Exp, bias=bh[:, m : m + 1])
+                ahead = c + WH_AHEAD
+                if ahead < WH_CHUNKS:
+                    wh_grouped = turn_wh(ahead, scalar_only)
+                for j in range(2):
+                    turn_wo(half, 2 * u2 + j)
                 nc.vector.tensor_scalar(
                     out=below[:], in0=below[:], scalar1=-1.0, scalar2=0.0, op0=ALU.add, op1=ALU.min
                 )
-                nc.vector.scalar_tensor_tensor(
-                    out=h2_rows[:, t, :],
-                    in0=pre_h[:],
-                    scalar=bh[:, m : m + 1],
-                    in1=below[:],
-                    op0=ALU.add,
-                    op1=ALU.max,
-                )
-            h2_grouped = stage.tile([P, BATCH, PACK], BF16, bufs=2, align_bytes=64)
-            nc.vector.tensor_copy(out=h2_grouped[:], in_=h2_rows[:].rearrange("p t b -> p b t"))
+                for e in range(2):
+                    m = 2 * c + e
+                    nc.vector.scalar_tensor_tensor(
+                        out=h2_rows[:, m % PACK, :],
+                        in0=pre_hs[e][:],
+                        scalar=bh[:, m : m + 1],
+                        in1=below[:, e, :],
+                        op0=ALU.add,
+                        op1=ALU.max,
+                    )
+                if ahead < WH_CHUNKS:
+                    quantise_wh(ahead, wh_grouped)
+            h2_grouped = stage.tile([P, BATCH, PACK], BF16, align_bytes=64)
+            nc.vector.tensor_copy(
+                out=h2_grouped[:].rearrange("p (n i) t -> p n t i", i=4),
+                in_=h2_rows[:].rearrange("p t (n i) -> p n t i", i=4),
+            )
+            return h2_grouped
+
+        def quantise_h2(g2, h2_grouped):
             nc.vector.quantize_mx(
                 out=h2_codes[:, g2, :].bitcast(FP8X4),
                 scales=h2_scales[:, g2, :],
                 in_=h2_grouped[:].rearrange("p b t -> p (b t)"),
             )
-
-        wo_codes = keep.tile([P, 2, PASSES, SAMPLE], U32, align_bytes=64)
-        wo_scales = keep.tile([P, 2, PASSES, SAMPLE], U8, align_bytes=64)
-
-        def quantise_wo(half):
-            wo_grouped = stage.tile([P, PASSES * SAMPLE * PACK], BF16, bufs=2, align_bytes=64)
-            for j in range(SAMPLE // P):
-                turned = turn_row_tile(nc, banks, identity, wo_rows[:, 4 * half + j, :])
-                nc.scalar.copy(
-                    out=words_view(wo_grouped)[:, :, j * P : (j + 1) * P, :],
-                    in_=by_pass_and_column(turned),
-                )
-            for g in range(PASSES):
-                nc.vector.quantize_mx(
-                    out=wo_codes[:, half, g, :].bitcast(FP8X4),
-                    scales=wo_scales[:, half, g, :],
-                    in_=wo_grouped[:, g * SAMPLE * PACK : (g + 1) * SAMPLE * PACK],
-                )
 
         def second_product(half, i):
             o_sum = sums.tile([P, SAMPLE], F32, tag="sum")
@@ -186,6 +215,13 @@ def tile_prior_pb_kernel(
                 )
             return o_sum
 
+        for c in range(WH_AHEAD):
+            quantise_wh(c, turn_wh(c, both))
+        h2_grouped = hidden_pass(0, STD)
+        quantise_wo(STD)
+        quantise_h2(0, h2_grouped)
+        quantise_h2(1, hidden_pass(1, MEAN))
+
         mean = keep.tile([P, BATCH_TILES, SAMPLE], F32)
         std_pre = keep.tile([P, BATCH_TILES, SAMPLE], F32)
         soft = keep.tile([P, BATCH_TILES, SAMPLE], F32)
@@ -195,35 +231,39 @@ def tile_prior_pb_kernel(
         std_dram = out_1.rearrange("(p i) s -> p i s", i=BATCH_TILES)
         sample_dram = out_2.rearrange("(p i) s -> p i s", i=BATCH_TILES)
 
-        quantise_wo(STD)
-        for i in range(BATCH_TILES):
-            o_sum = second_product(STD, i)
-            nc.vector.tensor_tensor(
-                out=std_pre[:, i, :], in0=o_sum[:], in1=bo_all[:, SAMPLE : 2 * SAMPLE], op=ALU.add
-            )
-            nc.scalar.activation(out=soft[:, i, :], in_=std_pre[:, i, :], func=ACT.Abs)
-            nc.scalar.activation(out=soft[:, i, :], in_=soft[:, i, :], func=ACT.Exp, scale=-1.0)
+        for pair in range(BATCH_TILES // 2):
+            tiles = (2 * pair, 2 * pair + 1)
+            for i in tiles:
+                o_sum = second_product(STD, i)
+                nc.vector.tensor_tensor(out=std_pre[:, i, :], in0=o_sum[:], in1=bo_all[:, STD, :], op=ALU.add)
+                nc.scalar.activation(out=soft[:, i, :], in_=std_pre[:, i, :], func=ACT.Abs)
+            for i in tiles:
+                nc.scalar.activation(out=soft[:, i, :], in_=soft[:, i, :], func=ACT.Exp, scale=-1.0)
 
         quantise_wo(MEAN)
         for i in range(BATCH_TILES):
             o_sum = second_product(MEAN, i)
-            nc.vector.tensor_tensor(out=mean[:, i, :], in0=o_sum[:], in1=bo_all[:, 0:SAMPLE], op=ALU.add)
+            nc.vector.tensor_tensor(out=mean[:, i, :], in0=o_sum[:], in1=bo_all[:, MEAN, :], op=ALU.add)
             nc.sync.dma_start(out=mean_dram[:, i, :], in_=mean[:, i, :])
 
         c_tenth = math.exp(0.1)
-        for i in range(BATCH_TILES):
-            nc.scalar.activation(
-                out=soft[:, i, :], in_=soft[:, i, :], func=ACT.Ln, scale=c_tenth, bias=c_tenth
-            )
-            nc.vector.scalar_tensor_tensor(
-                out=std[:, i, :],
-                in0=std_pre[:, i, :],
-                scalar=0.0,
-                in1=soft[:, i, :],
-                op0=ALU.max,
-                op1=ALU.add,
-            )
-            nc.sync.dma_start(out=std_dram[:, i, :], in_=std[:, i, :])
-            nc.vector.tensor_tensor(out=sample[:, i, :], in0=std[:, i, :], in1=eps_rows[:, i, :], op=ALU.mult)
-            nc.vector.tensor_tensor(out=sample[:, i, :], in0=sample[:, i, :], in1=mean[:, i, :], op=ALU.add)
-            nc.sync.dma_start(out=sample_dram[:, i, :], in_=sample[:, i, :])
+        for pair in range(BATCH_TILES // 2):
+            tiles = (2 * pair, 2 * pair + 1)
+            for i in tiles:
+                nc.scalar.activation(
+                    out=soft[:, i, :], in_=soft[:, i, :], func=ACT.Ln, scale=c_tenth, bias=c_tenth
+                )
+                nc.vector.scalar_tensor_tensor(
+                    out=std[:, i, :],
+                    in0=std_pre[:, i, :],
+                    scalar=0.0,
+                    in1=soft[:, i, :],
+                    op0=ALU.max,
+                    op1=ALU.add,
+                )
+                nc.sync.dma_start(out=std_dram[:, i, :], in_=std[:, i, :])
+            for i in tiles:
+                nc.vector.tensor_tensor(out=sample[:, i, :], in0=std[:, i, :], in1=eps_rows[:, i, :], op=ALU.mult)
+            for i in tiles:
+                nc.vector.tensor_tensor(out=sample[:, i, :], in0=sample[:, i, :], in1=mean[:, i, :], op=ALU.add)
+                nc.sync.dma_start(out=sample_dram[:, i, :], in_=sample[:, i, :])

@@ -21,21 +21,23 @@ SAMPLE = 512
 PASSES = DEPTH // (P * PACK)
 CHUNKS = DEPTH // 2 // P
 BATCH_TILES = BATCH // P
+HALF_BATCH = BATCH // 2
 HIDDEN_TILES = HIDDEN // P
 WH_CHUNKS = HIDDEN_TILES // 2
-WH_AHEAD = 2
+WO_CHUNKS = SAMPLE // P // 2
+AHEAD = 2
 MEAN = 0
 STD = 1
 
 FLOPS = 2 * BATCH * DEPTH * HIDDEN + 2 * BATCH * DEPTH * 2 * SAMPLE
 
 
-def turn_row_tile(nc, banks, identity, rows, grouped_words, copy_out):
+def turn_row_tile(nc, banks, identity, rows, grouped_words):
     words = rows.bitcast(F32)
     turned = banks.tile([P, CHUNKS, P], F32, tag="turned")
     for c in range(CHUNKS):
         nc.tensor.transpose(turned[:, c, :], words[:, c * P : (c + 1) * P], identity[:])
-    copy_out(out=grouped_words, in_=turned[:].rearrange("p (g u) r -> p g r u", u=2))
+    nc.scalar.copy(out=grouped_words, in_=turned[:].rearrange("p (g u) r -> p g r u", u=2))
 
 
 def words_view(grouped):
@@ -51,7 +53,6 @@ def tile_prior_pb_kernel(
         stage = ctx.enter_context(tc.tile_pool(name="stage", bufs=2))
         banks = ctx.enter_context(tc.psum_pool(name="banks", bufs=4))
         sums = ctx.enter_context(tc.psum_pool(name="sums", bufs=4))
-        ctx.enter_context(tc.manual_schedule())
 
         identity = keep.tile([P, P], F32)
         make_identity(nc, identity[:])
@@ -61,8 +62,8 @@ def tile_prior_pb_kernel(
 
         x_rows = keep.tile([P, BATCH_TILES, DEPTH], BF16)
         x_dram = rnn_hidden.rearrange("(p i) r -> p i r", i=BATCH_TILES)
-        for j in range(2):
-            nc.sync.dma_start(out=x_rows[:, 2 * j : 2 * j + 2, :], in_=x_dram[:, 2 * j : 2 * j + 2, :])
+        for i in range(BATCH_TILES):
+            nc.sync.dma_start(out=x_rows[:, i, :], in_=x_dram[:, i, :])
 
         wh_rows = keep.tile([P, HIDDEN_TILES, DEPTH], BF16)
         wh_dram = W_h.rearrange("(c p e) r -> p c e r", p=P, e=2)
@@ -77,129 +78,136 @@ def tile_prior_pb_kernel(
         wo_rows = keep.tile([P, 2, SAMPLE // P, DEPTH], BF16)
         wo_dram = W_out.rearrange("(f j p) h -> p f j h", f=2, p=P)
         for half in (STD, MEAN):
-            for j in range(2):
+            for c in range(WO_CHUNKS):
                 nc.sync.dma_start(
-                    out=wo_rows[:, half, 2 * j : 2 * j + 2, :], in_=wo_dram[:, half, 2 * j : 2 * j + 2, :]
+                    out=wo_rows[:, half, 2 * c : 2 * c + 2, :], in_=wo_dram[:, half, 2 * c : 2 * c + 2, :]
                 )
         eps_rows = keep.tile([P, BATCH_TILES, SAMPLE], BF16)
         nc.sync.dma_start(out=eps_rows[:], in_=eps.rearrange("(p i) s -> p i s", i=BATCH_TILES))
         bo_all = keep.tile([P, 2, SAMPLE], BF16)
         nc.sync.dma_start(out=bo_all[:].rearrange("p f s -> p (f s)"), in_=b_out.partition_broadcast(P))
 
-        both = (nc.scalar.copy, nc.vector.tensor_copy)
-        scalar_only = (nc.scalar.copy, nc.scalar.copy)
-
-        x_grouped = keep.tile([P, PASSES * BATCH * PACK], BF16, align_bytes=64)
+        x_grouped = keep.tile([P, PASSES, BATCH * PACK], BF16, align_bytes=64)
         x_codes = keep.tile([P, PASSES, BATCH], U32, align_bytes=64)
         x_scales = keep.tile([P, PASSES, BATCH], U8, align_bytes=64)
+        x_words = words_view(x_grouped[:].rearrange("p g n -> p (g n)"))
         for i in range(BATCH_TILES):
-            turn_row_tile(
-                nc, banks, identity, x_rows[:, i, :],
-                words_view(x_grouped[:])[:, :, i * P : (i + 1) * P, :], both[i % 2],
-            )
-        for g in range(PASSES):
-            nc.vector.quantize_mx(
-                out=x_codes[:, g, :].bitcast(FP8X4),
-                scales=x_scales[:, g, :],
-                in_=x_grouped[:, g * BATCH * PACK : (g + 1) * BATCH * PACK],
-            )
+            turn_row_tile(nc, banks, identity, x_rows[:, i, :], x_words[:, :, i * P : (i + 1) * P, :])
+        for i in range(BATCH_TILES):
+            for g in range(PASSES):
+                nc.vector.quantize_mx(
+                    out=x_codes[:, g, i * P : (i + 1) * P].bitcast(FP8X4),
+                    scales=x_scales[:, g, i * P : (i + 1) * P],
+                    in_=x_grouped[:, g, i * P * PACK : (i + 1) * P * PACK],
+                )
 
         bh = keep.tile([P, HIDDEN_TILES], F32)
         nc.vector.tensor_copy(out=bh[:], in_=bh_bf16[:])
 
+        wh_grouped = keep.tile([P, HIDDEN_TILES, PASSES * P * PACK], BF16, align_bytes=64)
         wh_codes = keep.tile([P, HIDDEN_TILES, PASSES * P], U32, align_bytes=64)
         wh_scales = keep.tile([P, HIDDEN_TILES, PASSES * P], U8, align_bytes=64)
-
-        def turn_wh(c, copiers):
-            wh_grouped = stage.tile([P, 2, PASSES * P * PACK], BF16, align_bytes=64)
-            for e in range(2):
-                turn_row_tile(
-                    nc, banks, identity, wh_rows[:, 2 * c + e, :], words_view(wh_grouped[:, e, :]), copiers[e]
-                )
-            return wh_grouped
-
-        def quantise_wh(c, wh_grouped):
-            nc.vector.quantize_mx(
-                out=wh_codes[:, 2 * c : 2 * c + 2, :].rearrange("p e n -> p (e n)").bitcast(FP8X4),
-                scales=wh_scales[:, 2 * c : 2 * c + 2, :].rearrange("p e n -> p (e n)"),
-                in_=wh_grouped[:].rearrange("p e n -> p (e n)"),
-            )
-
-        wo_grouped = keep.tile([P, 2, PASSES * SAMPLE * PACK], BF16, align_bytes=64)
+        wo_grouped = keep.tile([P, 2, PASSES, SAMPLE * PACK], BF16, align_bytes=64)
         wo_codes = keep.tile([P, 2, PASSES, SAMPLE], U32, align_bytes=64)
         wo_scales = keep.tile([P, 2, PASSES, SAMPLE], U8, align_bytes=64)
 
-        def turn_wo(half, j):
-            turn_row_tile(
-                nc, banks, identity, wo_rows[:, half, j, :],
-                words_view(wo_grouped[:, half, :])[:, :, j * P : (j + 1) * P, :], nc.scalar.copy,
-            )
+        def wo_chunk(k):
+            return (STD, MEAN)[(k - WH_CHUNKS) // WO_CHUNKS], (k - WH_CHUNKS) % WO_CHUNKS
 
-        def quantise_wo(half):
-            for g in range(PASSES):
-                nc.vector.quantize_mx(
-                    out=wo_codes[:, half, g, :].bitcast(FP8X4),
-                    scales=wo_scales[:, half, g, :],
-                    in_=wo_grouped[:, half, g * SAMPLE * PACK : (g + 1) * SAMPLE * PACK],
-                )
+        def turn_chunk(k):
+            for e in range(2):
+                if k < WH_CHUNKS:
+                    m = 2 * k + e
+                    turn_row_tile(nc, banks, identity, wh_rows[:, m, :], words_view(wh_grouped[:, m, :]))
+                else:
+                    half, c = wo_chunk(k)
+                    j = 2 * c + e
+                    wo_words = words_view(wo_grouped[:, half, :, :].rearrange("p g n -> p (g n)"))
+                    turn_row_tile(
+                        nc, banks, identity, wo_rows[:, half, j, :], wo_words[:, :, j * P : (j + 1) * P, :]
+                    )
 
+        def quantise_chunk(k):
+            for e in range(2):
+                if k < WH_CHUNKS:
+                    m = 2 * k + e
+                    nc.vector.quantize_mx(
+                        out=wh_codes[:, m, :].bitcast(FP8X4), scales=wh_scales[:, m, :], in_=wh_grouped[:, m, :]
+                    )
+                else:
+                    half, c = wo_chunk(k)
+                    g = e
+                    nc.vector.quantize_mx(
+                        out=wo_codes[:, half, g, 2 * c * P : (2 * c + 2) * P].bitcast(FP8X4),
+                        scales=wo_scales[:, half, g, 2 * c * P : (2 * c + 2) * P],
+                        in_=wo_grouped[:, half, g, 2 * c * P * PACK : (2 * c + 2) * P * PACK],
+                    )
+
+        h2_rows = keep.tile([P, PASSES, PACK, BATCH], BF16)
+        h2_grouped = keep.tile([P, PASSES, BATCH, PACK], BF16, align_bytes=64)
         h2_codes = keep.tile([P, PASSES, BATCH], U32, align_bytes=64)
         h2_scales = keep.tile([P, PASSES, BATCH], U8, align_bytes=64)
 
-        def hidden_pass(g2, half):
-            h2_rows = stage.tile([P, PACK, BATCH], BF16)
-            for u2 in range(2):
-                c = 2 * g2 + u2
-                below = stage.tile([P, 2, BATCH], F32)
-                pre_hs = []
-                for e in range(2):
-                    m = 2 * c + e
-                    pre_h = sums.tile([P, BATCH], F32, tag="sum")
-                    pre_hs.append(pre_h)
-                    for g in range(PASSES):
-                        nc.tensor.matmul_mx(
-                            out=pre_h[:],
-                            lhsT=wh_codes[:, m, g * P : (g + 1) * P].bitcast(FP8X4),
-                            lhsT_scale=wh_scales[:, m, g * P : (g + 1) * P],
-                            rhs=x_codes[:, g, :].bitcast(FP8X4),
-                            rhs_scale=x_scales[:, g, :],
-                            start=(g == 0),
-                            stop=(g == PASSES - 1),
-                        )
-                    nc.scalar.activation(out=below[:, e, :], in_=pre_h[:], func=ACT.Exp, bias=bh[:, m : m + 1])
-                ahead = c + WH_AHEAD
-                if ahead < WH_CHUNKS:
-                    wh_grouped = turn_wh(ahead, scalar_only)
-                for j in range(2):
-                    turn_wo(half, 2 * u2 + j)
-                nc.vector.tensor_scalar(
-                    out=below[:], in0=below[:], scalar1=-1.0, scalar2=0.0, op0=ALU.add, op1=ALU.min
-                )
-                for e in range(2):
-                    m = 2 * c + e
-                    nc.vector.scalar_tensor_tensor(
-                        out=h2_rows[:, m % PACK, :],
-                        in0=pre_hs[e][:],
-                        scalar=bh[:, m : m + 1],
-                        in1=below[:, e, :],
-                        op0=ALU.add,
-                        op1=ALU.max,
-                    )
-                if ahead < WH_CHUNKS:
-                    quantise_wh(ahead, wh_grouped)
-            h2_grouped = stage.tile([P, BATCH, PACK], BF16, align_bytes=64)
+        def regroup_h2(g2, hb):
+            cols = slice(hb * HALF_BATCH, (hb + 1) * HALF_BATCH)
             nc.vector.tensor_copy(
-                out=h2_grouped[:].rearrange("p (n i) t -> p n t i", i=4),
-                in_=h2_rows[:].rearrange("p t (n i) -> p n t i", i=4),
+                out=h2_grouped[:, g2, cols, :].rearrange("p (n i) t -> p n t i", i=4),
+                in_=h2_rows[:, g2, :, cols].rearrange("p t (n i) -> p n t i", i=4),
             )
-            return h2_grouped
 
-        def quantise_h2(g2, h2_grouped):
+        def quantise_h2(g2, hb):
+            cols = slice(hb * HALF_BATCH, (hb + 1) * HALF_BATCH)
             nc.vector.quantize_mx(
-                out=h2_codes[:, g2, :].bitcast(FP8X4),
-                scales=h2_scales[:, g2, :],
-                in_=h2_grouped[:].rearrange("p b t -> p (b t)"),
+                out=h2_codes[:, g2, cols].bitcast(FP8X4),
+                scales=h2_scales[:, g2, cols],
+                in_=h2_grouped[:, g2, cols, :].rearrange("p b t -> p (b t)"),
             )
+
+        for k in range(AHEAD):
+            turn_chunk(k)
+            quantise_chunk(k)
+        for c in range(WH_CHUNKS):
+            below = stage.tile([P, 2, BATCH], F32)
+            pre_hs = []
+            for e in range(2):
+                m = 2 * c + e
+                pre_h = sums.tile([P, BATCH], F32, tag="sum")
+                pre_hs.append(pre_h)
+                for g in range(PASSES):
+                    nc.tensor.matmul_mx(
+                        out=pre_h[:],
+                        lhsT=wh_codes[:, m, g * P : (g + 1) * P].bitcast(FP8X4),
+                        lhsT_scale=wh_scales[:, m, g * P : (g + 1) * P],
+                        rhs=x_codes[:, g, :].bitcast(FP8X4),
+                        rhs_scale=x_scales[:, g, :],
+                        start=(g == 0),
+                        stop=(g == PASSES - 1),
+                    )
+                nc.scalar.activation(out=below[:, e, :], in_=pre_h[:], func=ACT.Exp, bias=bh[:, m : m + 1])
+            turn_chunk(c + AHEAD)
+            nc.vector.tensor_scalar(
+                out=below[:], in0=below[:], scalar1=-1.0, scalar2=0.0, op0=ALU.add, op1=ALU.min
+            )
+            for e in range(2):
+                m = 2 * c + e
+                nc.vector.scalar_tensor_tensor(
+                    out=h2_rows[:, m // PACK, m % PACK, :],
+                    in0=pre_hs[e][:],
+                    scalar=bh[:, m : m + 1],
+                    in1=below[:, e, :],
+                    op0=ALU.add,
+                    op1=ALU.max,
+                )
+            pass_done = c % 2 == 1
+            if pass_done:
+                regroup_h2(c // 2, 0)
+            quantise_chunk(c + AHEAD)
+            if pass_done:
+                quantise_h2(c // 2, 0)
+                regroup_h2(c // 2, 1)
+                quantise_h2(c // 2, 1)
+        for k in range(WH_CHUNKS + AHEAD, WH_CHUNKS + 2 * WO_CHUNKS):
+            turn_chunk(k)
 
         def second_product(half, i):
             o_sum = sums.tile([P, SAMPLE], F32, tag="sum")
@@ -214,13 +222,6 @@ def tile_prior_pb_kernel(
                     stop=(g == PASSES - 1),
                 )
             return o_sum
-
-        for c in range(WH_AHEAD):
-            quantise_wh(c, turn_wh(c, both))
-        h2_grouped = hidden_pass(0, STD)
-        quantise_wo(STD)
-        quantise_h2(0, h2_grouped)
-        quantise_h2(1, hidden_pass(1, MEAN))
 
         mean = keep.tile([P, BATCH_TILES, SAMPLE], F32)
         std_pre = keep.tile([P, BATCH_TILES, SAMPLE], F32)
@@ -240,7 +241,8 @@ def tile_prior_pb_kernel(
             for i in tiles:
                 nc.scalar.activation(out=soft[:, i, :], in_=soft[:, i, :], func=ACT.Exp, scale=-1.0)
 
-        quantise_wo(MEAN)
+        for k in range(WH_CHUNKS + AHEAD, WH_CHUNKS + 2 * WO_CHUNKS):
+            quantise_chunk(k)
         for i in range(BATCH_TILES):
             o_sum = second_product(MEAN, i)
             nc.vector.tensor_tensor(out=mean[:, i, :], in0=o_sum[:], in1=bo_all[:, MEAN, :], op=ALU.add)

@@ -150,7 +150,8 @@ def tile_prior_pb_kernel(
 
         def regroup_h2(g2, hb):
             cols = slice(hb * HALF_BATCH, (hb + 1) * HALF_BATCH)
-            nc.vector.tensor_copy(
+            copy = (nc.vector.tensor_copy, nc.scalar.copy)[hb]
+            copy(
                 out=h2_grouped[:, g2, cols, :].rearrange("p (n i) t -> p n t i", i=4),
                 in_=h2_rows[:, g2, :, cols].rearrange("p t (n i) -> p n t i", i=4),
             )

@@ -186,11 +186,11 @@ def tile_prior_pb_kernel(
                     )
                 nc.scalar.activation(out=below[:, e, :], in_=pre_h[:], func=ACT.Exp, bias=bh[:, m : m + 1])
             turn_chunk(c + AHEAD)
-            nc.vector.tensor_scalar(
-                out=below[:], in0=below[:], scalar1=-1.0, scalar2=0.0, op0=ALU.add, op1=ALU.min
-            )
             for e in range(2):
                 m = 2 * c + e
+                nc.vector.tensor_scalar(
+                    out=below[:, e, :], in0=below[:, e, :], scalar1=-1.0, scalar2=0.0, op0=ALU.add, op1=ALU.min
+                )
                 nc.vector.scalar_tensor_tensor(
                     out=h2_rows[:, m // PACK, m % PACK, :],
                     in0=pre_hs[e][:],

@@ -28,6 +28,7 @@ WO_CHUNKS = SAMPLE // P // 2
 AHEAD = 2
 MEAN = 0
 STD = 1
+LARGE = 40.0
 
 FLOPS = 2 * BATCH * DEPTH * HIDDEN + 2 * BATCH * DEPTH * 2 * SAMPLE
 
@@ -86,6 +87,11 @@ def tile_prior_pb_kernel(
         nc.sync.dma_start(out=eps_rows[:], in_=eps.rearrange("(p i) s -> p i s", i=BATCH_TILES))
         bo_all = keep.tile([P, 2, SAMPLE], BF16)
         nc.sync.dma_start(out=bo_all[:].rearrange("p f s -> p (f s)"), in_=b_out.partition_broadcast(P))
+
+        bo_std = keep.tile([P, SAMPLE], F32)
+        nc.gpsimd.tensor_scalar(
+            out=bo_std[:], in0=bo_all[:, STD, :], scalar1=1.0, scalar2=0.1, op0=ALU.mult, op1=ALU.add
+        )
 
         x_grouped = keep.tile([P, PASSES, BATCH * PACK], BF16, align_bytes=64)
         x_codes = keep.tile([P, PASSES, BATCH], U32, align_bytes=64)
@@ -233,37 +239,26 @@ def tile_prior_pb_kernel(
         std_dram = out_1.rearrange("(p i) s -> p i s", i=BATCH_TILES)
         sample_dram = out_2.rearrange("(p i) s -> p i s", i=BATCH_TILES)
 
-        for pair in range(BATCH_TILES // 2):
-            tiles = (2 * pair, 2 * pair + 1)
-            for i in tiles:
+        with tc.manual_schedule(engines={mybir.EngineType.Activation}):
+            for i in range(BATCH_TILES):
                 o_sum = second_product(STD, i)
-                nc.vector.tensor_tensor(out=std_pre[:, i, :], in0=o_sum[:], in1=bo_all[:, STD, :], op=ALU.add)
-                nc.scalar.activation(out=soft[:, i, :], in_=std_pre[:, i, :], func=ACT.Abs)
-            for i in tiles:
-                nc.scalar.activation(out=soft[:, i, :], in_=soft[:, i, :], func=ACT.Exp, scale=-1.0)
-
-        for k in range(WH_CHUNKS + AHEAD, WH_CHUNKS + 2 * WO_CHUNKS):
-            quantise_chunk(k)
-        for i in range(BATCH_TILES):
-            o_sum = second_product(MEAN, i)
-            nc.vector.tensor_tensor(out=mean[:, i, :], in0=o_sum[:], in1=bo_all[:, MEAN, :], op=ALU.add)
-            nc.sync.dma_start(out=mean_dram[:, i, :], in_=mean[:, i, :])
-
-        c_tenth = math.exp(0.1)
+                nc.vector.tensor_tensor(out=std_pre[:, i, :], in0=o_sum[:], in1=bo_std[:], op=ALU.add)
+                nc.gpsimd.tensor_scalar(
+                    out=soft[:, i, :], in0=std_pre[:, i, :], scalar1=LARGE, scalar2=-LARGE, op0=ALU.min, op1=ALU.max
+                )
+                nc.scalar.activation(out=soft[:, i, :], in_=soft[:, i, :], func=ACT.Exp)
+            for k in range(WH_CHUNKS + AHEAD, WH_CHUNKS + 2 * WO_CHUNKS):
+                quantise_chunk(k)
+            for i in range(BATCH_TILES):
+                o_sum = second_product(MEAN, i)
+                nc.vector.tensor_tensor(out=mean[:, i, :], in0=o_sum[:], in1=bo_all[:, MEAN, :], op=ALU.add)
+                nc.sync.dma_start(out=mean_dram[:, i, :], in_=mean[:, i, :])
+            for i in range(BATCH_TILES):
+                nc.scalar.activation(out=soft[:, i, :], in_=soft[:, i, :], func=ACT.Ln, bias=math.exp(0.1))
         for pair in range(BATCH_TILES // 2):
             tiles = (2 * pair, 2 * pair + 1)
             for i in tiles:
-                nc.scalar.activation(
-                    out=soft[:, i, :], in_=soft[:, i, :], func=ACT.Ln, scale=c_tenth, bias=c_tenth
-                )
-                nc.vector.scalar_tensor_tensor(
-                    out=std[:, i, :],
-                    in0=std_pre[:, i, :],
-                    scalar=0.0,
-                    in1=soft[:, i, :],
-                    op0=ALU.max,
-                    op1=ALU.add,
-                )
+                nc.vector.tensor_tensor(out=std[:, i, :], in0=soft[:, i, :], in1=std_pre[:, i, :], op=ALU.max)
                 nc.sync.dma_start(out=std_dram[:, i, :], in_=std[:, i, :])
             for i in tiles:
                 nc.vector.tensor_tensor(out=sample[:, i, :], in0=std[:, i, :], in1=eps_rows[:, i, :], op=ALU.mult)

@@ -231,6 +231,7 @@ def tile_prior_pb_kernel(
             return o_sum
 
         mean = keep.tile([P, BATCH_TILES, SAMPLE], F32)
+        exp_w = keep.tile([P, BATCH_TILES, SAMPLE], F32)
         std_pre = keep.tile([P, BATCH_TILES, SAMPLE], F32)
         soft = keep.tile([P, BATCH_TILES, SAMPLE], F32)
         std = keep.tile([P, BATCH_TILES, SAMPLE], F32)
@@ -243,10 +244,10 @@ def tile_prior_pb_kernel(
             for i in range(BATCH_TILES):
                 o_sum = second_product(STD, i)
                 nc.vector.tensor_tensor(out=std_pre[:, i, :], in0=o_sum[:], in1=bo_std[:], op=ALU.add)
+                nc.scalar.activation(out=exp_w[:, i, :], in_=std_pre[:, i, :], func=ACT.Exp)
                 nc.gpsimd.tensor_scalar(
-                    out=soft[:, i, :], in0=std_pre[:, i, :], scalar1=LARGE, scalar2=-LARGE, op0=ALU.min, op1=ALU.max
+                    out=soft[:, i, :], in0=exp_w[:, i, :], scalar1=math.exp(LARGE), scalar2=0.0, op0=ALU.min, op1=ALU.max
                 )
-                nc.scalar.activation(out=soft[:, i, :], in_=soft[:, i, :], func=ACT.Exp)
             for k in range(WH_CHUNKS + AHEAD, WH_CHUNKS + 2 * WO_CHUNKS):
                 quantise_chunk(k)
             for i in range(BATCH_TILES):

@@ -28,6 +28,7 @@ WO_CHUNKS = SAMPLE // P // 2
 AHEAD = 2
 MEAN = 0
 STD = 1
+TENSOR_ADDS = 2
 LARGE = 40.0
 
 FLOPS = 2 * BATCH * DEPTH * HIDDEN + 2 * BATCH * DEPTH * 2 * SAMPLE
@@ -236,11 +237,12 @@ def tile_prior_pb_kernel(
         soft = keep.tile([P, BATCH_TILES, SAMPLE], F32)
         std = keep.tile([P, BATCH_TILES, SAMPLE], F32)
         sample = keep.tile([P, BATCH_TILES, SAMPLE], F32)
+        scaled = keep.tile([P, BATCH_TILES, SAMPLE], F32)
         mean_dram = out_0.rearrange("(p i) s -> p i s", i=BATCH_TILES)
         std_dram = out_1.rearrange("(p i) s -> p i s", i=BATCH_TILES)
         sample_dram = out_2.rearrange("(p i) s -> p i s", i=BATCH_TILES)
 
-        with tc.manual_schedule(engines={mybir.EngineType.Activation}):
+        with tc.manual_schedule(engines={mybir.EngineType.Activation, mybir.EngineType.PE}):
             for i in range(BATCH_TILES):
                 o_sum = second_product(STD, i)
                 nc.vector.tensor_tensor(out=std_pre[:, i, :], in0=o_sum[:], in1=bo_std[:], op=ALU.add)
@@ -256,13 +258,19 @@ def tile_prior_pb_kernel(
                 nc.sync.dma_start(out=mean_dram[:, i, :], in_=mean[:, i, :])
             for i in range(BATCH_TILES):
                 nc.scalar.activation(out=soft[:, i, :], in_=soft[:, i, :], func=ACT.Ln, bias=math.exp(0.1))
-        for pair in range(BATCH_TILES // 2):
-            tiles = (2 * pair, 2 * pair + 1)
-            for i in tiles:
+
+            both = []
+            for i in range(TENSOR_ADDS):
+                added = banks.tile([P, SAMPLE], F32, tag="turned")
+                both.append(added)
+                nc.tensor.matmul(out=added[:], lhsT=identity[:], rhs=mean[:, i, :], start=True, stop=False)
+            for i in range(BATCH_TILES):
                 nc.vector.tensor_tensor(out=std[:, i, :], in0=soft[:, i, :], in1=std_pre[:, i, :], op=ALU.max)
                 nc.sync.dma_start(out=std_dram[:, i, :], in_=std[:, i, :])
-            for i in tiles:
-                nc.vector.tensor_tensor(out=sample[:, i, :], in0=std[:, i, :], in1=eps_rows[:, i, :], op=ALU.mult)
-            for i in tiles:
-                nc.vector.tensor_tensor(out=sample[:, i, :], in0=sample[:, i, :], in1=mean[:, i, :], op=ALU.add)
+                nc.vector.tensor_tensor(out=scaled[:, i, :], in0=std[:, i, :], in1=eps_rows[:, i, :], op=ALU.mult)
+                if i < TENSOR_ADDS:
+                    nc.tensor.matmul(out=both[i][:], lhsT=identity[:], rhs=scaled[:, i, :], start=False, stop=True)
+                    nc.scalar.copy(out=sample[:, i, :], in_=both[i][:])
+                else:
+                    nc.vector.tensor_tensor(out=sample[:, i, :], in0=scaled[:, i, :], in1=mean[:, i, :], op=ALU.add)
                 nc.sync.dma_start(out=sample_dram[:, i, :], in_=sample[:, i, :])

@@ -34,12 +34,12 @@ LARGE = 40.0
 FLOPS = 2 * BATCH * DEPTH * HIDDEN + 2 * BATCH * DEPTH * 2 * SAMPLE
 
 
-def turn_row_tile(nc, banks, identity, rows, grouped_words):
+def turn_row_tile(nc, banks, identity, rows, grouped_words, copy):
     words = rows.bitcast(F32)
     turned = banks.tile([P, CHUNKS, P], F32, tag="turned")
     for c in range(CHUNKS):
         nc.tensor.transpose(turned[:, c, :], words[:, c * P : (c + 1) * P], identity[:])
-    nc.scalar.copy(out=grouped_words, in_=turned[:].rearrange("p (g u) r -> p g r u", u=2))
+    copy(out=grouped_words, in_=turned[:].rearrange("p (g u) r -> p g r u", u=2))
 
 
 def words_view(grouped):
@@ -70,12 +70,13 @@ def tile_prior_pb_kernel(
         wh_rows = keep.tile([P, HIDDEN_TILES, DEPTH], BF16)
         wh_dram = W_h.rearrange("(c p e) r -> p c e r", p=P, e=2)
         bh_bf16 = keep.tile([P, HIDDEN_TILES], BF16)
-        nc.scalar.dma_start(
-            out=bh_bf16[:].rearrange("p (c e) -> p c e", e=2),
-            in_=b_h.rearrange("(c p e) -> p c e", p=P, e=2),
-        )
         for c in range(WH_CHUNKS):
             nc.sync.dma_start(out=wh_rows[:, 2 * c : 2 * c + 2, :], in_=wh_dram[:, c, :, :])
+            if c == 0:
+                nc.sync.dma_start(
+                    out=bh_bf16[:].rearrange("p (c e) -> p c e", e=2),
+                    in_=b_h.rearrange("(c p e) -> p c e", p=P, e=2),
+                )
 
         wo_rows = keep.tile([P, 2, SAMPLE // P, DEPTH], BF16)
         wo_dram = W_out.rearrange("(f j p) h -> p f j h", f=2, p=P)
@@ -99,7 +100,8 @@ def tile_prior_pb_kernel(
         x_scales = keep.tile([P, PASSES, BATCH], U8, align_bytes=64)
         x_words = words_view(x_grouped[:].rearrange("p g n -> p (g n)"))
         for i in range(BATCH_TILES):
-            turn_row_tile(nc, banks, identity, x_rows[:, i, :], x_words[:, :, i * P : (i + 1) * P, :])
+            copy = (nc.scalar.copy, nc.vector.tensor_copy)[i % 2]
+            turn_row_tile(nc, banks, identity, x_rows[:, i, :], x_words[:, :, i * P : (i + 1) * P, :], copy)
         for i in range(BATCH_TILES):
             for g in range(PASSES):
                 nc.vector.quantize_mx(
@@ -125,13 +127,20 @@ def tile_prior_pb_kernel(
             for e in range(2):
                 if k < WH_CHUNKS:
                     m = 2 * k + e
-                    turn_row_tile(nc, banks, identity, wh_rows[:, m, :], words_view(wh_grouped[:, m, :]))
+                    turn_row_tile(
+                        nc, banks, identity, wh_rows[:, m, :], words_view(wh_grouped[:, m, :]), nc.scalar.copy
+                    )
                 else:
                     half, c = wo_chunk(k)
                     j = 2 * c + e
                     wo_words = words_view(wo_grouped[:, half, :, :].rearrange("p g n -> p (g n)"))
                     turn_row_tile(
-                        nc, banks, identity, wo_rows[:, half, j, :], wo_words[:, :, j * P : (j + 1) * P, :]
+                        nc,
+                        banks,
+                        identity,
+                        wo_rows[:, half, j, :],
+                        wo_words[:, :, j * P : (j + 1) * P, :],
+                        nc.scalar.copy,
                     )
 
         def quantise_chunk(k):

@@ -69,15 +69,16 @@ def tile_prior_pb_kernel(
 
         wh_rows = keep.tile([P, HIDDEN_TILES, DEPTH], BF16)
         wh_dram = W_h.rearrange("(c p e) r -> p c e r", p=P, e=2)
-        bh_bf16 = keep.tile([P, HIDDEN_TILES], BF16)
+        bh = keep.tile([P, HIDDEN_TILES], BF16)
         for c in range(WH_CHUNKS):
             nc.sync.dma_start(out=wh_rows[:, 2 * c : 2 * c + 2, :], in_=wh_dram[:, c, :, :])
             if c == 0:
                 nc.sync.dma_start(
-                    out=bh_bf16[:].rearrange("p (c e) -> p c e", e=2),
+                    out=bh[:].rearrange("p (c e) -> p c e", e=2),
                     in_=b_h.rearrange("(c p e) -> p c e", p=P, e=2),
                 )
 
+        bo_all = keep.tile([P, 2, SAMPLE], BF16)
         wo_rows = keep.tile([P, 2, SAMPLE // P, DEPTH], BF16)
         wo_dram = W_out.rearrange("(f j p) h -> p f j h", f=2, p=P)
         for half in (STD, MEAN):
@@ -85,10 +86,10 @@ def tile_prior_pb_kernel(
                 nc.sync.dma_start(
                     out=wo_rows[:, half, 2 * c : 2 * c + 2, :], in_=wo_dram[:, half, 2 * c : 2 * c + 2, :]
                 )
+            if half == STD:
+                nc.sync.dma_start(out=bo_all[:].rearrange("p f s -> p (f s)"), in_=b_out.partition_broadcast(P))
         eps_rows = keep.tile([P, BATCH_TILES, SAMPLE], BF16)
         nc.sync.dma_start(out=eps_rows[:], in_=eps.rearrange("(p i) s -> p i s", i=BATCH_TILES))
-        bo_all = keep.tile([P, 2, SAMPLE], BF16)
-        nc.sync.dma_start(out=bo_all[:].rearrange("p f s -> p (f s)"), in_=b_out.partition_broadcast(P))
 
         bo_std = keep.tile([P, SAMPLE], F32)
         nc.gpsimd.tensor_scalar(
@@ -109,9 +110,6 @@ def tile_prior_pb_kernel(
                     scales=x_scales[:, g, i * P : (i + 1) * P],
                     in_=x_grouped[:, g, i * P * PACK : (i + 1) * P * PACK],
                 )
-
-        bh = keep.tile([P, HIDDEN_TILES], F32)
-        nc.vector.tensor_copy(out=bh[:], in_=bh_bf16[:])
 
         wh_grouped = keep.tile([P, HIDDEN_TILES, PASSES * P * PACK], BF16, align_bytes=64)
         wh_codes = keep.tile([P, HIDDEN_TILES, PASSES * P], U32, align_bytes=64)

@@ -249,35 +249,43 @@ def tile_prior_pb_kernel(
         std_dram = out_1.rearrange("(p i) s -> p i s", i=BATCH_TILES)
         sample_dram = out_2.rearrange("(p i) s -> p i s", i=BATCH_TILES)
 
-        with tc.manual_schedule(engines={mybir.EngineType.Activation, mybir.EngineType.PE}):
-            for i in range(BATCH_TILES):
-                o_sum = second_product(STD, i)
-                nc.vector.tensor_tensor(out=std_pre[:, i, :], in0=o_sum[:], in1=bo_std[:], op=ALU.add)
-                nc.scalar.activation(out=exp_w[:, i, :], in_=std_pre[:, i, :], func=ACT.Exp)
-                nc.gpsimd.tensor_scalar(
-                    out=soft[:, i, :], in0=exp_w[:, i, :], scalar1=math.exp(LARGE), scalar2=0.0, op0=ALU.min, op1=ALU.max
-                )
-            for k in range(WH_CHUNKS + AHEAD, WH_CHUNKS + 2 * WO_CHUNKS):
-                quantise_chunk(k)
-            for i in range(BATCH_TILES):
-                o_sum = second_product(MEAN, i)
-                nc.vector.tensor_tensor(out=mean[:, i, :], in0=o_sum[:], in1=bo_all[:, MEAN, :], op=ALU.add)
-                nc.sync.dma_start(out=mean_dram[:, i, :], in_=mean[:, i, :])
-            for i in range(BATCH_TILES):
-                nc.scalar.activation(out=soft[:, i, :], in_=soft[:, i, :], func=ACT.Ln, bias=math.exp(0.1))
+        for i in range(BATCH_TILES):
+            o_sum = second_product(STD, i)
+            nc.vector.tensor_tensor(out=std_pre[:, i, :], in0=o_sum[:], in1=bo_std[:], op=ALU.add)
+            nc.scalar.activation(out=exp_w[:, i, :], in_=std_pre[:, i, :], func=ACT.Exp)
+            nc.gpsimd.tensor_scalar(
+                out=soft[:, i, :], in0=exp_w[:, i, :], scalar1=math.exp(LARGE), scalar2=0.0, op0=ALU.min, op1=ALU.max
+            )
+        tenth = keep.tile([P, 1], F32)
+        nc.gpsimd.tensor_scalar(
+            out=tenth[:],
+            in0=exp_w[:, BATCH_TILES - 1, 0:1],
+            scalar1=math.exp(0.1),
+            scalar2=math.exp(0.1),
+            op0=ALU.min,
+            op1=ALU.max,
+        )
+        for k in range(WH_CHUNKS + AHEAD, WH_CHUNKS + 2 * WO_CHUNKS):
+            quantise_chunk(k)
+        for i in range(BATCH_TILES):
+            o_sum = second_product(MEAN, i)
+            nc.vector.tensor_tensor(out=mean[:, i, :], in0=o_sum[:], in1=bo_all[:, MEAN, :], op=ALU.add)
+            nc.sync.dma_start(out=mean_dram[:, i, :], in_=mean[:, i, :])
+        for i in range(BATCH_TILES):
+            nc.scalar.activation(out=soft[:, i, :], in_=soft[:, i, :], func=ACT.Ln, bias=tenth[:])
 
-            both = []
-            for i in range(TENSOR_ADDS):
-                added = banks.tile([P, SAMPLE], F32, tag="turned")
-                both.append(added)
-                nc.tensor.matmul(out=added[:], lhsT=identity[:], rhs=mean[:, i, :], start=True, stop=False)
-            for i in range(BATCH_TILES):
-                nc.vector.tensor_tensor(out=std[:, i, :], in0=soft[:, i, :], in1=std_pre[:, i, :], op=ALU.max)
-                nc.sync.dma_start(out=std_dram[:, i, :], in_=std[:, i, :])
-                nc.vector.tensor_tensor(out=scaled[:, i, :], in0=std[:, i, :], in1=eps_rows[:, i, :], op=ALU.mult)
-                if i < TENSOR_ADDS:
-                    nc.tensor.matmul(out=both[i][:], lhsT=identity[:], rhs=scaled[:, i, :], start=False, stop=True)
-                    nc.scalar.copy(out=sample[:, i, :], in_=both[i][:])
-                else:
-                    nc.vector.tensor_tensor(out=sample[:, i, :], in0=scaled[:, i, :], in1=mean[:, i, :], op=ALU.add)
-                nc.sync.dma_start(out=sample_dram[:, i, :], in_=sample[:, i, :])
+        both = []
+        for i in range(TENSOR_ADDS):
+            added = banks.tile([P, SAMPLE], F32, tag="turned")
+            both.append(added)
+            nc.tensor.matmul(out=added[:], lhsT=identity[:], rhs=mean[:, i, :], start=True, stop=False)
+        for i in range(BATCH_TILES):
+            nc.vector.tensor_tensor(out=std[:, i, :], in0=soft[:, i, :], in1=std_pre[:, i, :], op=ALU.max)
+            nc.sync.dma_start(out=std_dram[:, i, :], in_=std[:, i, :])
+            nc.vector.tensor_tensor(out=scaled[:, i, :], in0=std[:, i, :], in1=eps_rows[:, i, :], op=ALU.mult)
+            if i < TENSOR_ADDS:
+                nc.tensor.matmul(out=both[i][:], lhsT=identity[:], rhs=scaled[:, i, :], start=False, stop=True)
+                nc.scalar.copy(out=sample[:, i, :], in_=both[i][:])
+            else:
+                nc.vector.tensor_tensor(out=sample[:, i, :], in0=scaled[:, i, :], in1=mean[:, i, :], op=ALU.add)
+            nc.sync.dma_start(out=sample_dram[:, i, :], in_=sample[:, i, :])

import math
from contextlib import ExitStack

import concourse.mybir as mybir
from concourse.masks import make_identity

F32 = mybir.dt.float32
BF16 = mybir.dt.bfloat16
U32 = mybir.dt.uint32
U8 = mybir.dt.uint8
FP8X4 = mybir.dt.float8_e4m3fn_x4
ACT = mybir.ActivationFunctionType
ALU = mybir.AluOpType

P = 128
PACK = 4
BATCH = 512
DEPTH = 1024
HIDDEN = 1024
SAMPLE = 512
PASSES = DEPTH // (P * PACK)
CHUNKS = DEPTH // 2 // P
BATCH_TILES = BATCH // P
HALF_BATCH = BATCH // 2
HIDDEN_TILES = HIDDEN // P
WH_CHUNKS = HIDDEN_TILES // 2
WO_CHUNKS = SAMPLE // P // 2
AHEAD = 2
MEAN = 0
STD = 1
TENSOR_ADDS = 2
LARGE = 40.0

FLOPS = 2 * BATCH * DEPTH * HIDDEN + 2 * BATCH * DEPTH * 2 * SAMPLE


def turn_row_tile(nc, banks, identity, rows, grouped_words, copy):
    words = rows.bitcast(F32)
    turned = banks.tile([P, CHUNKS, P], F32, tag="turned")
    for c in range(CHUNKS):
        nc.tensor.transpose(turned[:, c, :], words[:, c * P : (c + 1) * P], identity[:])
    copy(out=grouped_words, in_=turned[:].rearrange("p (g u) r -> p g r u", u=2))


def words_view(grouped):
    return grouped.bitcast(F32).rearrange("p (g n u) -> p g n u", g=PASSES, u=2)


def tile_prior_pb_kernel(
    tc, rnn_hidden, eps, W_h, b_h, W_out, b_out, out_0, out_1, out_2
):
    nc = tc.nc
    with ExitStack() as ctx:
        keep = ctx.enter_context(tc.tile_pool(name="keep", bufs=1))
        stage = ctx.enter_context(tc.tile_pool(name="stage", bufs=2))
        banks = ctx.enter_context(tc.psum_pool(name="banks", bufs=4))
        sums = ctx.enter_context(tc.psum_pool(name="sums", bufs=4))

        identity = keep.tile([P, P], F32)
        make_identity(nc, identity[:])
        warm = keep.tile([P, 1], F32)
        nc.vector.memset(warm[:], 0.0)
        nc.scalar.activation(out=warm[:], in_=warm[:], func=ACT.Exp)

        x_rows = keep.tile([P, BATCH_TILES, DEPTH], BF16)
        x_dram = rnn_hidden.rearrange("(p i) r -> p i r", i=BATCH_TILES)
        for i in range(BATCH_TILES):
            nc.sync.dma_start(out=x_rows[:, i, :], in_=x_dram[:, i, :])

        wh_rows = keep.tile([P, HIDDEN_TILES, DEPTH], BF16)
        wh_dram = W_h.rearrange("(c p e) r -> p c e r", p=P, e=2)
        bh = keep.tile([P, HIDDEN_TILES], BF16)
        for c in range(WH_CHUNKS):
            nc.sync.dma_start(out=wh_rows[:, 2 * c : 2 * c + 2, :], in_=wh_dram[:, c, :, :])
            if c == 0:
                nc.sync.dma_start(
                    out=bh[:].rearrange("p (c e) -> p c e", e=2),
                    in_=b_h.rearrange("(c p e) -> p c e", p=P, e=2),
                )

        bo_all = keep.tile([P, 2, SAMPLE], BF16)
        wo_rows = keep.tile([P, 2, SAMPLE // P, DEPTH], BF16)
        wo_dram = W_out.rearrange("(f j p) h -> p f j h", f=2, p=P)
        for half in (STD, MEAN):
            for c in range(WO_CHUNKS):
                nc.sync.dma_start(
                    out=wo_rows[:, half, 2 * c : 2 * c + 2, :], in_=wo_dram[:, half, 2 * c : 2 * c + 2, :]
                )
            if half == STD:
                nc.sync.dma_start(out=bo_all[:].rearrange("p f s -> p (f s)"), in_=b_out.partition_broadcast(P))
        eps_rows = keep.tile([P, BATCH_TILES, SAMPLE], BF16)
        nc.sync.dma_start(out=eps_rows[:], in_=eps.rearrange("(p i) s -> p i s", i=BATCH_TILES))

        bo_std = keep.tile([P, SAMPLE], F32)
        nc.gpsimd.tensor_scalar(
            out=bo_std[:], in0=bo_all[:, STD, :], scalar1=1.0, scalar2=0.1, op0=ALU.mult, op1=ALU.add
        )

        x_grouped = keep.tile([P, PASSES, BATCH * PACK], BF16, align_bytes=64)
        x_codes = keep.tile([P, PASSES, BATCH], U32, align_bytes=64)
        x_scales = keep.tile([P, PASSES, BATCH], U8, align_bytes=64)
        x_words = words_view(x_grouped[:].rearrange("p g n -> p (g n)"))
        for i in range(BATCH_TILES):
            copy = (nc.scalar.copy, nc.vector.tensor_copy)[i % 2]
            turn_row_tile(nc, banks, identity, x_rows[:, i, :], x_words[:, :, i * P : (i + 1) * P, :], copy)
        for i in range(BATCH_TILES):
            for g in range(PASSES):
                nc.vector.quantize_mx(
                    out=x_codes[:, g, i * P : (i + 1) * P].bitcast(FP8X4),
                    scales=x_scales[:, g, i * P : (i + 1) * P],
                    in_=x_grouped[:, g, i * P * PACK : (i + 1) * P * PACK],
                )

        wh_grouped = keep.tile([P, HIDDEN_TILES, PASSES * P * PACK], BF16, align_bytes=64)
        wh_codes = keep.tile([P, HIDDEN_TILES, PASSES * P], U32, align_bytes=64)
        wh_scales = keep.tile([P, HIDDEN_TILES, PASSES * P], U8, align_bytes=64)
        wo_grouped = keep.tile([P, 2, PASSES, SAMPLE * PACK], BF16, align_bytes=64)
        wo_codes = keep.tile([P, 2, PASSES, SAMPLE], U32, align_bytes=64)
        wo_scales = keep.tile([P, 2, PASSES, SAMPLE], U8, align_bytes=64)

        def wo_chunk(k):
            return (STD, MEAN)[(k - WH_CHUNKS) // WO_CHUNKS], (k - WH_CHUNKS) % WO_CHUNKS

        def turn_chunk(k):
            for e in range(2):
                if k < WH_CHUNKS:
                    m = 2 * k + e
                    turn_row_tile(
                        nc, banks, identity, wh_rows[:, m, :], words_view(wh_grouped[:, m, :]), nc.scalar.copy
                    )
                else:
                    half, c = wo_chunk(k)
                    j = 2 * c + e
                    wo_words = words_view(wo_grouped[:, half, :, :].rearrange("p g n -> p (g n)"))
                    turn_row_tile(
                        nc,
                        banks,
                        identity,
                        wo_rows[:, half, j, :],
                        wo_words[:, :, j * P : (j + 1) * P, :],
                        nc.scalar.copy,
                    )

        def quantise_chunk(k):
            for e in range(2):
                if k < WH_CHUNKS:
                    m = 2 * k + e
                    nc.vector.quantize_mx(
                        out=wh_codes[:, m, :].bitcast(FP8X4), scales=wh_scales[:, m, :], in_=wh_grouped[:, m, :]
                    )
                else:
                    half, c = wo_chunk(k)
                    g = e
                    nc.vector.quantize_mx(
                        out=wo_codes[:, half, g, 2 * c * P : (2 * c + 2) * P].bitcast(FP8X4),
                        scales=wo_scales[:, half, g, 2 * c * P : (2 * c + 2) * P],
                        in_=wo_grouped[:, half, g, 2 * c * P * PACK : (2 * c + 2) * P * PACK],
                    )

        h2_rows = keep.tile([P, PASSES, PACK, BATCH], BF16)
        h2_grouped = keep.tile([P, PASSES, BATCH, PACK], BF16, align_bytes=64)
        h2_codes = keep.tile([P, PASSES, BATCH], U32, align_bytes=64)
        h2_scales = keep.tile([P, PASSES, BATCH], U8, align_bytes=64)

        def regroup_h2(g2, hb):
            cols = slice(hb * HALF_BATCH, (hb + 1) * HALF_BATCH)
            copy = (nc.vector.tensor_copy, nc.scalar.copy)[hb]
            copy(
                out=h2_grouped[:, g2, cols, :].rearrange("p (n i) t -> p n t i", i=4),
                in_=h2_rows[:, g2, :, cols].rearrange("p t (n i) -> p n t i", i=4),
            )

        def quantise_h2(g2, hb):
            cols = slice(hb * HALF_BATCH, (hb + 1) * HALF_BATCH)
            nc.vector.quantize_mx(
                out=h2_codes[:, g2, cols].bitcast(FP8X4),
                scales=h2_scales[:, g2, cols],
                in_=h2_grouped[:, g2, cols, :].rearrange("p b t -> p (b t)"),
            )

        for k in range(AHEAD):
            turn_chunk(k)
            quantise_chunk(k)
        for c in range(WH_CHUNKS):
            below = stage.tile([P, 2, BATCH], F32)
            pre_hs = []
            for e in range(2):
                m = 2 * c + e
                pre_h = sums.tile([P, BATCH], F32, tag="sum")
                pre_hs.append(pre_h)
                for g in range(PASSES):
                    nc.tensor.matmul_mx(
                        out=pre_h[:],
                        lhsT=wh_codes[:, m, g * P : (g + 1) * P].bitcast(FP8X4),
                        lhsT_scale=wh_scales[:, m, g * P : (g + 1) * P],
                        rhs=x_codes[:, g, :].bitcast(FP8X4),
                        rhs_scale=x_scales[:, g, :],
                        start=(g == 0),
                        stop=(g == PASSES - 1),
                    )
                nc.scalar.activation(out=below[:, e, :], in_=pre_h[:], func=ACT.Exp, bias=bh[:, m : m + 1])
            turn_chunk(c + AHEAD)
            for e in range(2):
                m = 2 * c + e
                nc.vector.tensor_scalar(
                    out=below[:, e, :], in0=below[:, e, :], scalar1=-1.0, scalar2=0.0, op0=ALU.add, op1=ALU.min
                )
                nc.vector.scalar_tensor_tensor(
                    out=h2_rows[:, m // PACK, m % PACK, :],
                    in0=pre_hs[e][:],
                    scalar=bh[:, m : m + 1],
                    in1=below[:, e, :],
                    op0=ALU.add,
                    op1=ALU.max,
                )
            pass_done = c % 2 == 1
            if pass_done:
                regroup_h2(c // 2, 0)
            quantise_chunk(c + AHEAD)
            if pass_done:
                quantise_h2(c // 2, 0)
                regroup_h2(c // 2, 1)
                quantise_h2(c // 2, 1)
        for k in range(WH_CHUNKS + AHEAD, WH_CHUNKS + 2 * WO_CHUNKS):
            turn_chunk(k)

        def second_product(half, i):
            o_sum = sums.tile([P, SAMPLE], F32, tag="sum")
            for g in range(PASSES):
                nc.tensor.matmul_mx(
                    out=o_sum[:],
                    lhsT=h2_codes[:, g, i * P : (i + 1) * P].bitcast(FP8X4),
                    lhsT_scale=h2_scales[:, g, i * P : (i + 1) * P],
                    rhs=wo_codes[:, half, g, :].bitcast(FP8X4),
                    rhs_scale=wo_scales[:, half, g, :],
                    start=(g == 0),
                    stop=(g == PASSES - 1),
                )
            return o_sum

        mean = keep.tile([P, BATCH_TILES, SAMPLE], F32)
        exp_w = keep.tile([P, BATCH_TILES, SAMPLE], F32)
        std_pre = keep.tile([P, BATCH_TILES, SAMPLE], F32)
        soft = keep.tile([P, BATCH_TILES, SAMPLE], F32)
        std = keep.tile([P, BATCH_TILES, SAMPLE], F32)
        sample = keep.tile([P, BATCH_TILES, SAMPLE], F32)
        scaled = keep.tile([P, BATCH_TILES, SAMPLE], F32)
        mean_dram = out_0.rearrange("(p i) s -> p i s", i=BATCH_TILES)
        std_dram = out_1.rearrange("(p i) s -> p i s", i=BATCH_TILES)
        sample_dram = out_2.rearrange("(p i) s -> p i s", i=BATCH_TILES)

        for i in range(BATCH_TILES):
            o_sum = second_product(STD, i)
            nc.vector.tensor_tensor(out=std_pre[:, i, :], in0=o_sum[:], in1=bo_std[:], op=ALU.add)
            nc.scalar.activation(out=exp_w[:, i, :], in_=std_pre[:, i, :], func=ACT.Exp)
            nc.gpsimd.tensor_scalar(
                out=soft[:, i, :], in0=exp_w[:, i, :], scalar1=math.exp(LARGE), scalar2=0.0, op0=ALU.min, op1=ALU.max
            )
        tenth = keep.tile([P, 1], F32)
        nc.gpsimd.tensor_scalar(
            out=tenth[:],
            in0=exp_w[:, BATCH_TILES - 1, 0:1],
            scalar1=math.exp(0.1),
            scalar2=math.exp(0.1),
            op0=ALU.min,
            op1=ALU.max,
        )
        for k in range(WH_CHUNKS + AHEAD, WH_CHUNKS + 2 * WO_CHUNKS):
            quantise_chunk(k)
        for i in range(BATCH_TILES):
            o_sum = second_product(MEAN, i)
            nc.vector.tensor_tensor(out=mean[:, i, :], in0=o_sum[:], in1=bo_all[:, MEAN, :], op=ALU.add)
            nc.sync.dma_start(out=mean_dram[:, i, :], in_=mean[:, i, :])
        for i in range(BATCH_TILES):
            nc.scalar.activation(out=soft[:, i, :], in_=soft[:, i, :], func=ACT.Ln, bias=tenth[:])

        both = []
        for i in range(TENSOR_ADDS):
            added = banks.tile([P, SAMPLE], F32, tag="turned")
            both.append(added)
            nc.tensor.matmul(out=added[:], lhsT=identity[:], rhs=mean[:, i, :], start=True, stop=False)
        for i in range(BATCH_TILES):
            nc.vector.tensor_tensor(out=std[:, i, :], in0=soft[:, i, :], in1=std_pre[:, i, :], op=ALU.max)
            nc.sync.dma_start(out=std_dram[:, i, :], in_=std[:, i, :])
            nc.vector.tensor_tensor(out=scaled[:, i, :], in0=std[:, i, :], in1=eps_rows[:, i, :], op=ALU.mult)
            if i < TENSOR_ADDS:
                nc.tensor.matmul(out=both[i][:], lhsT=identity[:], rhs=scaled[:, i, :], start=False, stop=True)
                nc.scalar.copy(out=sample[:, i, :], in_=both[i][:])
            else:
                nc.vector.tensor_tensor(out=sample[:, i, :], in0=scaled[:, i, :], in1=mean[:, i, :], op=ALU.add)
            nc.sync.dma_start(out=sample_dram[:, i, :], in_=sample[:, i, :])
